import numpy as np
import ml_dtypes


def mxq(x, axis, fmt="e4m3"):
    dtype, down = {"e4m3": (ml_dtypes.float8_e4m3fn, 7), "e5m2": (ml_dtypes.float8_e5m2, 14)}[fmt]
    v = np.moveaxis(np.asarray(x, np.float32).astype(ml_dtypes.bfloat16).astype(np.float64), axis, -1)
    blocks = v.reshape(v.shape[:-1] + (-1, 32))
    amax = np.abs(blocks).max(-1, keepdims=True)
    byte = np.maximum(np.where(amax > 0, np.frexp(amax)[1] - 1 + 127, 0) - down, 1)
    scale = np.exp2(byte - 127.0)
    codes = (blocks / scale).astype(np.float32).astype(dtype).astype(np.float64)
    return np.moveaxis((codes * scale).reshape(v.shape), -1, axis)


WIDE = False


def mx_kscale(k):
    if not WIDE:
        return np.ones(k)
    levels = np.array([10, -10, 5, -5, 0])
    a = np.random.permutation(np.resize(levels, k // 512 * 4)).reshape(k // 512, 4)
    idx = np.arange(k)
    return np.exp2(a[idx // 512, idx % 128 // 32])


BF16 = ml_dtypes.bfloat16


def bf(x):
    return np.asarray(x, np.float32).astype(BF16)


def f64(x):
    return np.asarray(x).astype(np.float64)


E2M1 = np.array([0.0, 0.5, 1.0, 1.5, 2.0, 3.0, 4.0, 6.0, -0.0, -0.5, -1.0, -1.5, -2.0, -3.0, -4.0, -6.0])


def pack_weight(w, fmt):
    k, n = w.shape
    w = f64(bf(w)).reshape(k // 32, 32, n)
    amax = np.abs(w).max(1)
    if fmt == "e4m3":
        byte = np.frexp(amax)[1] - 1 + 127 - 7
    else:
        mant, ex = np.frexp(amax / 6.0)
        byte = np.where(mant > 0.5, ex, ex - 1) + 127
    byte = np.clip(np.where(amax > 0, byte, 1), 1, 254)
    scaled = (w * np.exp2(127.0 - byte)[:, None, :]).reshape(k, n).astype(np.float32)
    by_word = np.ascontiguousarray(scaled.reshape(k // 512, 128, 4, n).transpose(0, 1, 3, 2))
    if fmt == "e4m3":
        words = by_word.astype(ml_dtypes.float8_e4m3fn).view(np.uint8)
    else:
        c = by_word.astype(ml_dtypes.float4_e2m1fn).view(np.uint8) & 0xF
        words = c[..., 0::2] | (c[..., 1::2] << 4)
    return np.ascontiguousarray(words), np.ascontiguousarray(byte.astype(np.uint8).reshape(k // 512, 16, n))


def unpack_weight(words, scales, fmt):
    g, p, n, _ = words.shape
    if fmt == "e4m3":
        vals = np.ascontiguousarray(words).view(ml_dtypes.float8_e4m3fn).astype(np.float64)
    else:
        nib = np.empty((g, p, n, 4), np.uint8)
        nib[..., 0::2] = words & 0xF
        nib[..., 1::2] = words >> 4
        vals = E2M1[nib]
    vals = vals * np.repeat(np.exp2(scales.astype(np.float64) - 127.0), 8, axis=1)[..., None]
    return vals.transpose(0, 1, 3, 2).reshape(g * 512, n)


B, C, PS, G, E = 128, 3, 64, 4, 256
NP = G * G
M1 = NP // 2
K2 = 2 * E
FMT = "e4m3"


def setup_inputs():
    t = mx_kscale(K2)[:E]
    tt = np.concatenate([t, t])
    h1 = bf(np.random.standard_normal((B, NP, M1, E)) * t)
    cross_w = np.random.standard_normal((E, K2)) / np.sqrt(K2) * t[:, None] / tt[None, :]
    words, scales = pack_weight(np.ascontiguousarray(cross_w.T), FMT)
    cross_b = bf(np.random.standard_normal(E) * 0.3 * t)
    return {"h1": h1,
            "cross_w_words": words,
            "cross_w_scales": scales,
            "cross_b": cross_b}


def reference(h1, cross_w_words, cross_w_scales, cross_b):
    wt = unpack_weight(cross_w_words, cross_w_scales, FMT)
    bias = f64(cross_b)
    g1 = f64(h1).reshape(B, NP, M1 // 2, K2)
    h2 = (mxq(g1, 3, "e4m3") @ wt) + bias
    g2 = h2.reshape(B, NP, M1 // 4, K2)
    return (mxq(g2, 3, "e4m3") @ wt) + bias

@@ -1,0 +1,213 @@
+from contextlib import ExitStack
+
+import concourse.mybir as mybir
+from concourse.masks import make_identity
+
+F32 = mybir.dt.float32
+BF16 = mybir.dt.bfloat16
+I32 = mybir.dt.int32
+U32 = mybir.dt.uint32
+U8 = mybir.dt.uint8
+FP8X4 = mybir.dt.float8_e4m3fn_x4
+ADD = mybir.AluOpType.add
+
+P = 128
+E = 256
+K = 2 * E
+TILES = 32
+PAIR = 2
+ROUNDS = TILES // PAIR
+
+FLOPS = 2 * 8192 * K * E + 2 * 4096 * K * E
+
+
+def tile_simplemodel_pc_t_kernel(tc, h1, cross_w_words, cross_w_scales, cross_b, out):
+    nc = tc.nc
+    h1_rows = h1.rearrange("b i m e -> b (i m e)")
+    out_rows = out.rearrange("b i m e -> b (i m e)")
+
+    with ExitStack() as ctx:
+        consts = ctx.enter_context(tc.tile_pool(name="consts", bufs=1))
+        x_pool = ctx.enter_context(tc.tile_pool(name="x", bufs=ROUNDS))
+        work = ctx.enter_context(tc.tile_pool(name="work", bufs=3))
+        o_pool = ctx.enter_context(tc.tile_pool(name="o", bufs=4))
+        ps_xt = ctx.enter_context(tc.psum_pool(name="ps_xt", bufs=2 * PAIR))
+        ps_acc1 = ctx.enter_context(tc.psum_pool(name="ps_acc1", bufs=PAIR))
+        ps_ht = ctx.enter_context(tc.psum_pool(name="ps_ht", bufs=1))
+        ps_acc2 = ctx.enter_context(tc.psum_pool(name="ps_acc2", bufs=1))
+
+        ctx.enter_context(tc.manual_schedule())
+
+        x_tiles = []
+        w_codes = consts.tile([P, E], U32, align_bytes=64)
+        w_scales = consts.tile([P, E], U8, align_bytes=64)
+        nc.vector.memset(w_scales[:].bitcast(I32), 0)
+        for r in range(ROUNDS):
+            x_r = x_pool.tile([P, PAIR * 2 * K], BF16, name="x")
+            nc.sync.dma_start(out=x_r[:], in_=h1_rows[:, r * PAIR * 2 * K : (r + 1) * PAIR * 2 * K])
+            x_tiles.append(x_r)
+            if r == 0:
+                nc.sync.dma_start(
+                    out=w_codes[:].bitcast(I32),
+                    in_=cross_w_words[0].rearrange("p n t -> p (n t)").bitcast(I32),
+                )
+                for j in range(4):
+                    nc.sync.dma_start(
+                        out=w_scales[j : P : 32, :].bitcast(I32),
+                        in_=cross_w_scales[0, j : 16 : 4, :].bitcast(I32),
+                    )
+
+        ident = consts.tile([P, P], F32)
+        make_identity(nc, ident[:])
+        ones = consts.tile([P, P], BF16)
+        nc.vector.memset(ones[:], 1.0)
+        b_row = consts.tile([P, E], BF16)
+        nc.vector.memset(b_row[:], 0.0)
+        nc.scalar.dma_start(out=b_row[0:1, :], in_=cross_b.unsqueeze(0))
+        b_ps = ps_acc2.tile([P, PAIR, E], F32, name="acc2")
+        nc.tensor.matmul(out=b_ps[:, 0, :], lhsT=ones[:], rhs=b_row[:], start=True, stop=True)
+        bias_nat = consts.tile([P, E], F32)
+        nc.vector.tensor_copy(out=bias_nat[:], in_=b_ps[:, 0, :])
+        bias_srt = consts.tile([P, 2, P, 2], F32)
+        for half in range(2):
+            nc.vector.tensor_copy(
+                out=bias_srt[:, :, half * 64 : (half + 1) * 64, :],
+                in_=b_ps[:, 0, :].rearrange("c (j u e) -> c u j e", u=2, e=2),
+            )
+
+        live = {}
+
+        def transpose_g1(r):
+            for s in range(PAIR):
+                xt = ps_xt.tile([P, 2, 2, P], F32, name="xt")
+                words = x_tiles[r][:, s * 2 * K : (s + 1) * 2 * K].bitcast(F32)
+                for par in range(2):
+                    for u in range(2):
+                        nc.tensor.transpose(
+                            xt[:, par, u, :], words[:, par * E + u : (par + 1) * E : 2], ident[:]
+                        )
+                live["xt", r, s] = xt
+
+        def group_g1(r):
+            g1 = work.tile([P, PAIR, 2, P, 4], BF16, name="g1", align_bytes=64)
+            for s in range(PAIR):
+                nc.scalar.copy(
+                    out=g1[:, s, :, :, :].bitcast(F32),
+                    in_=live["xt", r, s][:].rearrange("p a u c -> p a c u"),
+                )
+            live["g1", r] = g1
+
+        def quantise_g1(r):
+            c1 = work.tile([P, PAIR * 2 * P], U32, name="c1", align_bytes=64)
+            s1 = work.tile([P, PAIR * 2 * P], U8, name="s1", align_bytes=64)
+            nc.vector.quantize_mx(
+                out=c1[:].bitcast(FP8X4),
+                scales=s1[:],
+                in_=live["g1", r][:].rearrange("p s a c t -> p (s a c t)"),
+            )
+            live["q1", r] = (c1, s1)
+
+        def level_one(r):
+            c1, s1 = live["q1", r]
+            for s in range(PAIR):
+                acc1 = ps_acc1.tile([P, K], F32, name="acc1")
+                for par in range(2):
+                    cols = slice((s * 2 + par) * P, (s * 2 + par + 1) * P)
+                    nc.tensor.matmul_mx(
+                        out=acc1[:, par * E : (par + 1) * E],
+                        lhsT=c1[:, cols].bitcast(FP8X4),
+                        lhsT_scale=s1[:, cols],
+                        rhs=w_codes[:].bitcast(FP8X4),
+                        rhs_scale=w_scales[:],
+                        start=True,
+                        stop=True,
+                    )
+                live["acc1", r, s] = acc1
+
+        def bias_and_round(r):
+            hs = work.tile([P, PAIR, 2, 2 * P], BF16, name="hs")
+            for s in range(PAIR):
+                nc.vector.tensor_tensor(
+                    out=hs[:, s, :, :].rearrange("c u (p e) -> c u p e", e=2),
+                    in0=live["acc1", r, s][:].rearrange("c (p u e) -> c u p e", u=2, e=2),
+                    in1=bias_srt[:],
+                    op=ADD,
+                )
+            live["hs", r] = hs
+
+        def transpose_g2(r):
+            hs = live["hs", r]
+            ht = ps_ht.tile([P, PAIR, 2, P], F32, name="ht")
+            for s in range(PAIR):
+                for u in range(2):
+                    nc.tensor.transpose(ht[:, s, u, :], hs[:, s, u, :].bitcast(F32), ident[:])
+            live["ht", r] = ht
+
+        def group_g2(r):
+            g2 = work.tile([P, PAIR, P, 4], BF16, name="g2", align_bytes=64)
+            nc.scalar.copy(
+                out=g2[:].bitcast(F32), in_=live["ht", r][:].rearrange("p s u c -> p s c u")
+            )
+            live["g2", r] = g2
+
+        def quantise_g2(r):
+            c2 = work.tile([P, PAIR * P], U32, name="c2", align_bytes=64)
+            s2 = work.tile([P, PAIR * P], U8, name="s2", align_bytes=64)
+            nc.vector.quantize_mx(
+                out=c2[:].bitcast(FP8X4),
+                scales=s2[:],
+                in_=live["g2", r][:].rearrange("p s c t -> p (s c t)"),
+            )
+            live["q2", r] = (c2, s2)
+
+        def level_two(r):
+            c2, s2 = live["q2", r]
+            acc2 = ps_acc2.tile([P, PAIR, E], F32, name="acc2")
+            for s in range(PAIR):
+                cols = slice(s * P, (s + 1) * P)
+                nc.tensor.matmul_mx(
+                    out=acc2[:, s, :],
+                    lhsT=c2[:, cols].bitcast(FP8X4),
+                    lhsT_scale=s2[:, cols],
+                    rhs=w_codes[:].bitcast(FP8X4),
+                    rhs_scale=w_scales[:],
+                    start=True,
+                    stop=True,
+                )
+            live["acc2", r] = acc2
+
+        def bias_and_store(r):
+            o = o_pool.tile([P, PAIR, E], F32, name="o")
+            nc.vector.tensor_tensor(
+                out=o[:],
+                in0=live["acc2", r][:],
+                in1=bias_nat[:].unsqueeze(1).to_broadcast([P, PAIR, E]),
+                op=ADD,
+            )
+            nc.sync.dma_start(
+                out=out_rows[:, r * PAIR * E : (r + 1) * PAIR * E],
+                in_=o[:].rearrange("c s n -> c (s n)"),
+            )
+
+        def in_range(r):
+            return 0 <= r < ROUNDS
+
+        for k in range(ROUNDS + 3):
+            if in_range(k):
+                transpose_g1(k)
+                group_g1(k)
+            if in_range(k - 2):
+                transpose_g2(k - 2)
+                group_g2(k - 2)
+            if in_range(k - 1):
+                level_one(k - 1)
+            if in_range(k - 3):
+                level_two(k - 3)
+            if in_range(k):
+                quantise_g1(k)
+            if in_range(k - 1):
+                bias_and_round(k - 1)
+            if in_range(k - 2):
+                quantise_g2(k - 2)
+            if in_range(k - 3):
+                bias_and_store(k - 3)

@@ -17,6 +17,7 @@ K = 2 * E
 TILES = 32
 PAIR = 2
 ROUNDS = TILES // PAIR
+LAG = 2
 
 FLOPS = 2 * 8192 * K * E + 2 * 4096 * K * E
 
@@ -29,12 +30,12 @@ def tile_simplemodel_pc_t_kernel(tc, h1, cross_w_words, cross_w_scales, cross_b,
     with ExitStack() as ctx:
         consts = ctx.enter_context(tc.tile_pool(name="consts", bufs=1))
         x_pool = ctx.enter_context(tc.tile_pool(name="x", bufs=ROUNDS))
-        work = ctx.enter_context(tc.tile_pool(name="work", bufs=3))
+        work = ctx.enter_context(tc.tile_pool(name="work", bufs=LAG + 2))
         o_pool = ctx.enter_context(tc.tile_pool(name="o", bufs=4))
-        ps_xt = ctx.enter_context(tc.psum_pool(name="ps_xt", bufs=2 * PAIR))
+        ps_xt = ctx.enter_context(tc.psum_pool(name="ps_xt", bufs=PAIR))
         ps_acc1 = ctx.enter_context(tc.psum_pool(name="ps_acc1", bufs=PAIR))
-        ps_ht = ctx.enter_context(tc.psum_pool(name="ps_ht", bufs=1))
-        ps_acc2 = ctx.enter_context(tc.psum_pool(name="ps_acc2", bufs=1))
+        ps_ht = ctx.enter_context(tc.psum_pool(name="ps_ht", bufs=2))
+        ps_acc2 = ctx.enter_context(tc.psum_pool(name="ps_acc2", bufs=2))
 
         ctx.enter_context(tc.manual_schedule())
 
@@ -192,22 +193,22 @@ def tile_simplemodel_pc_t_kernel(tc, h1, cross_w_words, cross_w_scales, cross_b,
         def in_range(r):
             return 0 <= r < ROUNDS
 
-        for k in range(ROUNDS + 3):
+        for k in range(ROUNDS + 3 * LAG):
             if in_range(k):
                 transpose_g1(k)
                 group_g1(k)
-            if in_range(k - 2):
-                transpose_g2(k - 2)
-                group_g2(k - 2)
-            if in_range(k - 1):
-                level_one(k - 1)
-            if in_range(k - 3):
-                level_two(k - 3)
+            if in_range(k - 2 * LAG):
+                transpose_g2(k - 2 * LAG)
+                group_g2(k - 2 * LAG)
+            if in_range(k - LAG):
+                level_one(k - LAG)
+            if in_range(k - 3 * LAG):
+                level_two(k - 3 * LAG)
+            if in_range(k - LAG):
+                bias_and_round(k - LAG)
+            if in_range(k - 3 * LAG):
+                bias_and_store(k - 3 * LAG)
             if in_range(k):
                 quantise_g1(k)
-            if in_range(k - 1):
-                bias_and_round(k - 1)
-            if in_range(k - 2):
-                quantise_g2(k - 2)
-            if in_range(k - 3):
-                bias_and_store(k - 3)
+            if in_range(k - 2 * LAG):
+                quantise_g2(k - 2 * LAG)

@@ -177,11 +177,16 @@ def tile_simplemodel_pc_t_kernel(tc, h1, cross_w_words, cross_w_scales, cross_b,
                 )
             live["acc2", r] = acc2
 
-        def bias_and_store(r):
+        def empty_level_two(r):
             o = o_pool.tile([P, PAIR, E], F32, name="o")
-            nc.vector.tensor_tensor(
+            nc.scalar.copy(out=o[:], in_=live["acc2", r][:])
+            live["o", r] = o
+
+        def bias_and_store(r):
+            o = live["o", r]
+            nc.gpsimd.tensor_tensor(
                 out=o[:],
-                in0=live["acc2", r][:],
+                in0=o[:],
                 in1=bias_nat[:].unsqueeze(1).to_broadcast([P, PAIR, E]),
                 op=ADD,
             )
@@ -204,10 +209,10 @@ def tile_simplemodel_pc_t_kernel(tc, h1, cross_w_words, cross_w_scales, cross_b,
                 level_one(k - LAG)
             if in_range(k - 3 * LAG):
                 level_two(k - 3 * LAG)
+                empty_level_two(k - 3 * LAG)
+                bias_and_store(k - 3 * LAG)
             if in_range(k - LAG):
                 bias_and_round(k - LAG)
-            if in_range(k - 3 * LAG):
-                bias_and_store(k - 3 * LAG)
             if in_range(k):
                 quantise_g1(k)
             if in_range(k - 2 * LAG):

@@ -17,6 +17,7 @@ K = 2 * E
 TILES = 32
 PAIR = 2
 ROUNDS = TILES // PAIR
+BANKS = 8
 LAG = 2
 
 FLOPS = 2 * 8192 * K * E + 2 * 4096 * K * E
@@ -29,13 +30,10 @@ def tile_simplemodel_pc_t_kernel(tc, h1, cross_w_words, cross_w_scales, cross_b,
 
     with ExitStack() as ctx:
         consts = ctx.enter_context(tc.tile_pool(name="consts", bufs=1))
-        x_pool = ctx.enter_context(tc.tile_pool(name="x", bufs=ROUNDS))
+        x_pool = ctx.enter_context(tc.tile_pool(name="x", bufs=TILES))
         work = ctx.enter_context(tc.tile_pool(name="work", bufs=LAG + 2))
         o_pool = ctx.enter_context(tc.tile_pool(name="o", bufs=4))
-        ps_xt = ctx.enter_context(tc.psum_pool(name="ps_xt", bufs=PAIR))
-        ps_acc1 = ctx.enter_context(tc.psum_pool(name="ps_acc1", bufs=PAIR))
-        ps_ht = ctx.enter_context(tc.psum_pool(name="ps_ht", bufs=2))
-        ps_acc2 = ctx.enter_context(tc.psum_pool(name="ps_acc2", bufs=2))
+        psum = ctx.enter_context(tc.psum_pool(name="psum", bufs=BANKS))
 
         ctx.enter_context(tc.manual_schedule())
 
@@ -43,11 +41,11 @@ def tile_simplemodel_pc_t_kernel(tc, h1, cross_w_words, cross_w_scales, cross_b,
         w_codes = consts.tile([P, E], U32, align_bytes=64)
         w_scales = consts.tile([P, E], U8, align_bytes=64)
         nc.vector.memset(w_scales[:].bitcast(I32), 0)
-        for r in range(ROUNDS):
-            x_r = x_pool.tile([P, PAIR * 2 * K], BF16, name="x")
-            nc.sync.dma_start(out=x_r[:], in_=h1_rows[:, r * PAIR * 2 * K : (r + 1) * PAIR * 2 * K])
-            x_tiles.append(x_r)
-            if r == 0:
+        for i in range(TILES):
+            x_i = x_pool.tile([P, 2 * K], BF16, name="x")
+            nc.sync.dma_start(out=x_i[:], in_=h1_rows[:, i * 2 * K : (i + 1) * 2 * K])
+            x_tiles.append(x_i)
+            if i == 0:
                 nc.sync.dma_start(
                     out=w_codes[:].bitcast(I32),
                     in_=cross_w_words[0].rearrange("p n t -> p (n t)").bitcast(I32),
@@ -65,7 +63,7 @@ def tile_simplemodel_pc_t_kernel(tc, h1, cross_w_words, cross_w_scales, cross_b,
         b_row = consts.tile([P, E], BF16)
         nc.vector.memset(b_row[:], 0.0)
         nc.scalar.dma_start(out=b_row[0:1, :], in_=cross_b.unsqueeze(0))
-        b_ps = ps_acc2.tile([P, PAIR, E], F32, name="acc2")
+        b_ps = psum.tile([P, PAIR, E], F32, name="b_ps", tag="bank")
         nc.tensor.matmul(out=b_ps[:, 0, :], lhsT=ones[:], rhs=b_row[:], start=True, stop=True)
         bias_nat = consts.tile([P, E], F32)
         nc.vector.tensor_copy(out=bias_nat[:], in_=b_ps[:, 0, :])
@@ -80,8 +78,8 @@ def tile_simplemodel_pc_t_kernel(tc, h1, cross_w_words, cross_w_scales, cross_b,
 
         def transpose_g1(r):
             for s in range(PAIR):
-                xt = ps_xt.tile([P, 2, 2, P], F32, name="xt")
-                words = x_tiles[r][:, s * 2 * K : (s + 1) * 2 * K].bitcast(F32)
+                xt = psum.tile([P, 2, 2, P], F32, name="xt", tag="bank")
+                words = x_tiles[r * PAIR + s][:].bitcast(F32)
                 for par in range(2):
                     for u in range(2):
                         nc.tensor.transpose(
@@ -111,7 +109,7 @@ def tile_simplemodel_pc_t_kernel(tc, h1, cross_w_words, cross_w_scales, cross_b,
         def level_one(r):
             c1, s1 = live["q1", r]
             for s in range(PAIR):
-                acc1 = ps_acc1.tile([P, K], F32, name="acc1")
+                acc1 = psum.tile([P, K], F32, name="acc1", tag="bank")
                 for par in range(2):
                     cols = slice((s * 2 + par) * P, (s * 2 + par + 1) * P)
                     nc.tensor.matmul_mx(
@@ -138,7 +136,7 @@ def tile_simplemodel_pc_t_kernel(tc, h1, cross_w_words, cross_w_scales, cross_b,
 
         def transpose_g2(r):
             hs = live["hs", r]
-            ht = ps_ht.tile([P, PAIR, 2, P], F32, name="ht")
+            ht = psum.tile([P, PAIR, 2, P], F32, name="ht", tag="bank")
             for s in range(PAIR):
                 for u in range(2):
                     nc.tensor.transpose(ht[:, s, u, :], hs[:, s, u, :].bitcast(F32), ident[:])
@@ -163,7 +161,7 @@ def tile_simplemodel_pc_t_kernel(tc, h1, cross_w_words, cross_w_scales, cross_b,
 
         def level_two(r):
             c2, s2 = live["q2", r]
-            acc2 = ps_acc2.tile([P, PAIR, E], F32, name="acc2")
+            acc2 = psum.tile([P, PAIR, E], F32, name="acc2", tag="bank")
             for s in range(PAIR):
                 cols = slice(s * P, (s + 1) * P)
                 nc.tensor.matmul_mx(
@@ -177,19 +175,14 @@ def tile_simplemodel_pc_t_kernel(tc, h1, cross_w_words, cross_w_scales, cross_b,
                 )
             live["acc2", r] = acc2
 
-        def empty_level_two(r):
-            o = o_pool.tile([P, PAIR, E], F32, name="o")
-            nc.scalar.copy(out=o[:], in_=live["acc2", r][:])
-            live["o", r] = o
-
         def bias_and_store(r):
-            o = live["o", r]
-            nc.gpsimd.tensor_tensor(
-                out=o[:],
-                in0=o[:],
-                in1=bias_nat[:].unsqueeze(1).to_broadcast([P, PAIR, E]),
-                op=ADD,
-            )
+            o = o_pool.tile([P, PAIR, E], F32, name="o")
+            bias = bias_nat[:].unsqueeze(1).to_broadcast([P, PAIR, E])
+            if r < ROUNDS - 2 * LAG:
+                nc.scalar.copy(out=o[:], in_=live["acc2", r][:])
+                nc.gpsimd.tensor_tensor(out=o[:], in0=o[:], in1=bias, op=ADD)
+            else:
+                nc.vector.tensor_tensor(out=o[:], in0=live["acc2", r][:], in1=bias, op=ADD)
             nc.sync.dma_start(
                 out=out_rows[:, r * PAIR * E : (r + 1) * PAIR * E],
                 in_=o[:].rearrange("c s n -> c (s n)"),
@@ -209,7 +202,6 @@ def tile_simplemodel_pc_t_kernel(tc, h1, cross_w_words, cross_w_scales, cross_b,
                 level_one(k - LAG)
             if in_range(k - 3 * LAG):
                 level_two(k - 3 * LAG)
-                empty_level_two(k - 3 * LAG)
                 bias_and_store(k - 3 * LAG)
             if in_range(k - LAG):
                 bias_and_round(k - LAG)

@@ -32,7 +32,7 @@ def tile_simplemodel_pc_t_kernel(tc, h1, cross_w_words, cross_w_scales, cross_b,
         consts = ctx.enter_context(tc.tile_pool(name="consts", bufs=1))
         x_pool = ctx.enter_context(tc.tile_pool(name="x", bufs=TILES))
         work = ctx.enter_context(tc.tile_pool(name="work", bufs=LAG + 2))
-        o_pool = ctx.enter_context(tc.tile_pool(name="o", bufs=4))
+        o_pool = ctx.enter_context(tc.tile_pool(name="o", bufs=8))
         psum = ctx.enter_context(tc.psum_pool(name="psum", bufs=BANKS))
 
         ctx.enter_context(tc.manual_schedule())

from contextlib import ExitStack

import concourse.mybir as mybir
from concourse.masks import make_identity

F32 = mybir.dt.float32
BF16 = mybir.dt.bfloat16
I32 = mybir.dt.int32
U32 = mybir.dt.uint32
U8 = mybir.dt.uint8
FP8X4 = mybir.dt.float8_e4m3fn_x4
ADD = mybir.AluOpType.add

P = 128
E = 256
K = 2 * E
TILES = 32
PAIR = 2
ROUNDS = TILES // PAIR
BANKS = 8
LAG = 2

FLOPS = 2 * 8192 * K * E + 2 * 4096 * K * E


def tile_simplemodel_pc_t_kernel(tc, h1, cross_w_words, cross_w_scales, cross_b, out):
    nc = tc.nc
    h1_rows = h1.rearrange("b i m e -> b (i m e)")
    out_rows = out.rearrange("b i m e -> b (i m e)")

    with ExitStack() as ctx:
        consts = ctx.enter_context(tc.tile_pool(name="consts", bufs=1))
        x_pool = ctx.enter_context(tc.tile_pool(name="x", bufs=TILES))
        work = ctx.enter_context(tc.tile_pool(name="work", bufs=LAG + 2))
        o_pool = ctx.enter_context(tc.tile_pool(name="o", bufs=8))
        psum = ctx.enter_context(tc.psum_pool(name="psum", bufs=BANKS))

        ctx.enter_context(tc.manual_schedule())

        x_tiles = []
        w_codes = consts.tile([P, E], U32, align_bytes=64)
        w_scales = consts.tile([P, E], U8, align_bytes=64)
        nc.vector.memset(w_scales[:].bitcast(I32), 0)
        for i in range(TILES):
            x_i = x_pool.tile([P, 2 * K], BF16, name="x")
            nc.sync.dma_start(out=x_i[:], in_=h1_rows[:, i * 2 * K : (i + 1) * 2 * K])
            x_tiles.append(x_i)
            if i == 0:
                nc.sync.dma_start(
                    out=w_codes[:].bitcast(I32),
                    in_=cross_w_words[0].rearrange("p n t -> p (n t)").bitcast(I32),
                )
                for j in range(4):
                    nc.sync.dma_start(
                        out=w_scales[j : P : 32, :].bitcast(I32),
                        in_=cross_w_scales[0, j : 16 : 4, :].bitcast(I32),
                    )

        ident = consts.tile([P, P], F32)
        make_identity(nc, ident[:])
        ones = consts.tile([P, P], BF16)
        nc.vector.memset(ones[:], 1.0)
        b_row = consts.tile([P, E], BF16)
        nc.vector.memset(b_row[:], 0.0)
        nc.scalar.dma_start(out=b_row[0:1, :], in_=cross_b.unsqueeze(0))
        b_ps = psum.tile([P, PAIR, E], F32, name="b_ps", tag="bank")
        nc.tensor.matmul(out=b_ps[:, 0, :], lhsT=ones[:], rhs=b_row[:], start=True, stop=True)
        bias_nat = consts.tile([P, E], F32)
        nc.vector.tensor_copy(out=bias_nat[:], in_=b_ps[:, 0, :])
        bias_srt = consts.tile([P, 2, P, 2], F32)
        for half in range(2):
            nc.vector.tensor_copy(
                out=bias_srt[:, :, half * 64 : (half + 1) * 64, :],
                in_=b_ps[:, 0, :].rearrange("c (j u e) -> c u j e", u=2, e=2),
            )

        live = {}

        def transpose_g1(r):
            for s in range(PAIR):
                xt = psum.tile([P, 2, 2, P], F32, name="xt", tag="bank")
                words = x_tiles[r * PAIR + s][:].bitcast(F32)
                for par in range(2):
                    for u in range(2):
                        nc.tensor.transpose(
                            xt[:, par, u, :], words[:, par * E + u : (par + 1) * E : 2], ident[:]
                        )
                live["xt", r, s] = xt

        def group_g1(r):
            g1 = work.tile([P, PAIR, 2, P, 4], BF16, name="g1", align_bytes=64)
            for s in range(PAIR):
                nc.scalar.copy(
                    out=g1[:, s, :, :, :].bitcast(F32),
                    in_=live["xt", r, s][:].rearrange("p a u c -> p a c u"),
                )
            live["g1", r] = g1

        def quantise_g1(r):
            c1 = work.tile([P, PAIR * 2 * P], U32, name="c1", align_bytes=64)
            s1 = work.tile([P, PAIR * 2 * P], U8, name="s1", align_bytes=64)
            nc.vector.quantize_mx(
                out=c1[:].bitcast(FP8X4),
                scales=s1[:],
                in_=live["g1", r][:].rearrange("p s a c t -> p (s a c t)"),
            )
            live["q1", r] = (c1, s1)

        def level_one(r):
            c1, s1 = live["q1", r]
            for s in range(PAIR):
                acc1 = psum.tile([P, K], F32, name="acc1", tag="bank")
                for par in range(2):
                    cols = slice((s * 2 + par) * P, (s * 2 + par + 1) * P)
                    nc.tensor.matmul_mx(
                        out=acc1[:, par * E : (par + 1) * E],
                        lhsT=c1[:, cols].bitcast(FP8X4),
                        lhsT_scale=s1[:, cols],
                        rhs=w_codes[:].bitcast(FP8X4),
                        rhs_scale=w_scales[:],
                        start=True,
                        stop=True,
                    )
                live["acc1", r, s] = acc1

        def bias_and_round(r):
            hs = work.tile([P, PAIR, 2, 2 * P], BF16, name="hs")
            for s in range(PAIR):
                nc.vector.tensor_tensor(
                    out=hs[:, s, :, :].rearrange("c u (p e) -> c u p e", e=2),
                    in0=live["acc1", r, s][:].rearrange("c (p u e) -> c u p e", u=2, e=2),
                    in1=bias_srt[:],
                    op=ADD,
                )
            live["hs", r] = hs

        def transpose_g2(r):
            hs = live["hs", r]
            ht = psum.tile([P, PAIR, 2, P], F32, name="ht", tag="bank")
            for s in range(PAIR):
                for u in range(2):
                    nc.tensor.transpose(ht[:, s, u, :], hs[:, s, u, :].bitcast(F32), ident[:])
            live["ht", r] = ht

        def group_g2(r):
            g2 = work.tile([P, PAIR, P, 4], BF16, name="g2", align_bytes=64)
            nc.scalar.copy(
                out=g2[:].bitcast(F32), in_=live["ht", r][:].rearrange("p s u c -> p s c u")
            )
            live["g2", r] = g2

        def quantise_g2(r):
            c2 = work.tile([P, PAIR * P], U32, name="c2", align_bytes=64)
            s2 = work.tile([P, PAIR * P], U8, name="s2", align_bytes=64)
            nc.vector.quantize_mx(
                out=c2[:].bitcast(FP8X4),
                scales=s2[:],
                in_=live["g2", r][:].rearrange("p s c t -> p (s c t)"),
            )
            live["q2", r] = (c2, s2)

        def level_two(r):
            c2, s2 = live["q2", r]
            acc2 = psum.tile([P, PAIR, E], F32, name="acc2", tag="bank")
            for s in range(PAIR):
                cols = slice(s * P, (s + 1) * P)
                nc.tensor.matmul_mx(
                    out=acc2[:, s, :],
                    lhsT=c2[:, cols].bitcast(FP8X4),
                    lhsT_scale=s2[:, cols],
                    rhs=w_codes[:].bitcast(FP8X4),
                    rhs_scale=w_scales[:],
                    start=True,
                    stop=True,
                )
            live["acc2", r] = acc2

        def bias_and_store(r):
            o = o_pool.tile([P, PAIR, E], F32, name="o")
            bias = bias_nat[:].unsqueeze(1).to_broadcast([P, PAIR, E])
            if r < ROUNDS - 2 * LAG:
                nc.scalar.copy(out=o[:], in_=live["acc2", r][:])
                nc.gpsimd.tensor_tensor(out=o[:], in0=o[:], in1=bias, op=ADD)
            else:
                nc.vector.tensor_tensor(out=o[:], in0=live["acc2", r][:], in1=bias, op=ADD)
            nc.sync.dma_start(
                out=out_rows[:, r * PAIR * E : (r + 1) * PAIR * E],
                in_=o[:].rearrange("c s n -> c (s n)"),
            )

        def in_range(r):
            return 0 <= r < ROUNDS

        for k in range(ROUNDS + 3 * LAG):
            if in_range(k):
                transpose_g1(k)
                group_g1(k)
            if in_range(k - 2 * LAG):
                transpose_g2(k - 2 * LAG)
                group_g2(k - 2 * LAG)
            if in_range(k - LAG):
                level_one(k - LAG)
            if in_range(k - 3 * LAG):
                level_two(k - 3 * LAG)
                bias_and_store(k - 3 * LAG)
            if in_range(k - LAG):
                bias_and_round(k - LAG)
            if in_range(k):
                quantise_g1(k)
            if in_range(k - 2 * LAG):
                quantise_g2(k - 2 * LAG)
